import numpy as np
import ml_dtypes


def mxq(x, axis, fmt="e4m3"):
    dtype, down = {"e4m3": (ml_dtypes.float8_e4m3fn, 7), "e5m2": (ml_dtypes.float8_e5m2, 14)}[fmt]
    v = np.moveaxis(np.asarray(x, np.float32).astype(ml_dtypes.bfloat16).astype(np.float64), axis, -1)
    blocks = v.reshape(v.shape[:-1] + (-1, 32))
    amax = np.abs(blocks).max(-1, keepdims=True)
    byte = np.maximum(np.where(amax > 0, np.frexp(amax)[1] - 1 + 127, 0) - down, 1)
    scale = np.exp2(byte - 127.0)
    codes = (blocks / scale).astype(np.float32).astype(dtype).astype(np.float64)
    return np.moveaxis((codes * scale).reshape(v.shape), -1, axis)


WIDE = False


def mx_kscale(k):
    if not WIDE:
        return np.ones(k)
    levels = np.array([10, -10, 5, -5, 0])
    a = np.random.permutation(np.resize(levels, k // 512 * 4)).reshape(k // 512, 4)
    idx = np.arange(k)
    return np.exp2(a[idx // 512, idx % 128 // 32])


BF16 = ml_dtypes.bfloat16


def bf(x):
    return np.asarray(x, np.float32).astype(BF16)


def f64(x):
    return np.asarray(x).astype(np.float64)


B, N, E, H, C = 4, 1024, 1024, 4, 512
D = E // H
EPS = 1e-5


def silu(t):
    return t / (1.0 + np.exp(-t))


def setup_inputs():
    t = mx_kscale(E)
    ret = np.random.standard_normal((B, N, H, D)) * 4.0 + np.random.standard_normal((B, N, H, 1)) * 2.0
    return {"ret": bf(ret.reshape(B, N, E)),
            "g": bf(np.random.standard_normal((B, N, E))),
            "gn_weight": bf((1.0 + 0.1 * np.random.standard_normal(E)) * t),
            "gn_bias": bf(0.1 * np.random.standard_normal(E) * t),
            "w_o": bf(np.random.standard_normal((E, E)) / np.sqrt(E) / t[:, None]),
            "b_o": bf(np.random.standard_normal(E) * 0.3)}


def reference(ret, g, gn_weight, gn_bias, w_o, b_o):
    r = f64(ret).reshape(B, N, H, D)
    mean = r.mean(axis=-1, keepdims=True)
    var = r.var(axis=-1, keepdims=True)
    r = (r - mean) / np.sqrt(var + EPS)
    rn = r.reshape(B, N, E) * f64(gn_weight) + f64(gn_bias)
    gate = silu(f64(g)) * rn
    return (mxq(gate, 2, "e4m3") @ mxq(f64(w_o), 0, "e4m3")) + f64(b_o)

@@ -1,0 +1,231 @@
+from contextlib import ExitStack
+
+import concourse.mybir as mybir
+from concourse.masks import make_identity
+
+F32 = mybir.dt.float32
+BF16 = mybir.dt.bfloat16
+U32 = mybir.dt.uint32
+U8 = mybir.dt.uint8
+FP8X4 = mybir.dt.float8_e4m3fn_x4
+ALU = mybir.AluOpType
+ACT = mybir.ActivationFunctionType
+
+P = 128
+PACK = 4
+K_PASS = P * PACK
+TOKENS = 4 * 1024
+E = 1024
+HEADS = 4
+HEAD = E // HEADS
+EPS = 1e-5
+PASSES = E // K_PASS
+K_BLOCKS = E // P
+TILES = 2
+TOK = TILES * P
+ROUNDS = TOKENS // TOK
+GROUPS = TILES * HEADS
+N_BANK = 512
+N_HALVES = E // N_BANK
+W_PIECES = 4
+
+FLOPS = 2 * TOKENS * E * E
+
+
+def tile_multiscaleretention_pc_t_kernel(tc, ret, g, gn_weight, gn_bias, w_o, b_o, out):
+    nc = tc.nc
+    ret_rounds = ret.flatten_outer_dims().rearrange("(r p j) c -> r p j c", p=P, j=TILES)
+    g_rounds = g.flatten_outer_dims().rearrange("(r p j) c -> r p j c", p=P, j=TILES)
+    out_rounds = out.flatten_outer_dims().rearrange("(r p j) c -> r p j c", p=P, j=TILES)
+    w_passes = w_o.rearrange("(c t p) n -> c p t n", t=PACK, p=P)
+
+    with ExitStack() as ctx:
+        const = ctx.enter_context(tc.tile_pool(name="const", bufs=1))
+        w_stage = ctx.enter_context(tc.tile_pool(name="w_stage", bufs=2))
+        x_pool = ctx.enter_context(tc.tile_pool(name="x", bufs=4))
+        g_pool = ctx.enter_context(tc.tile_pool(name="g", bufs=4))
+        small = ctx.enter_context(tc.tile_pool(name="small", bufs=4))
+        r_pool = ctx.enter_context(tc.tile_pool(name="r", bufs=3))
+        t_pool = ctx.enter_context(tc.tile_pool(name="transposed", bufs=5))
+        q_pool = ctx.enter_context(tc.tile_pool(name="quantised", bufs=3))
+        o_pool = ctx.enter_context(tc.tile_pool(name="o", bufs=3))
+        psum_r = ctx.enter_context(tc.psum_pool(name="psum_r", bufs=4))
+        psum_g = ctx.enter_context(tc.psum_pool(name="psum_g", bufs=2))
+        psum_o = ctx.enter_context(tc.psum_pool(name="psum_o", bufs=2))
+
+        x_of, g_of, mean_var_of, rstd_of, r_of, rn_of, silu_of, codes_of, scales_of = (
+            {}, {}, {}, {}, {}, {}, {}, {}, {},
+        )
+
+        def load_ret(r):
+            x_sb = x_pool.tile([P, TILES, E], BF16, name="x_sb")
+            nc.sync.dma_start(out=x_sb[:], in_=ret_rounds[r])
+            x_of[r] = x_sb
+
+        def load_g(r):
+            g_sb = g_pool.tile([P, TILES, E], BF16, name="g_sb")
+            nc.sync.dma_start(out=g_sb[:], in_=g_rounds[r])
+            g_of[r] = g_sb
+
+        def statistics(r):
+            x_sb = x_of[r]
+            stats = small.tile([P, GROUPS, 6], F32, name="stats")
+            mean_var = small.tile([P, GROUPS, 2], F32, name="mean_var")
+            for j in range(TILES):
+                for h in range(HEADS):
+                    i = j * HEADS + h
+                    nc.vector.bn_stats(out=stats[:, i, :], in_=x_sb[:, j, h * HEAD : (h + 1) * HEAD])
+                    nc.vector.bn_aggr(out=mean_var[:, i, :], in_=stats[:, i, :])
+            var_eps = small.tile([P, GROUPS], F32, name="var_eps")
+            nc.gpsimd.tensor_scalar(
+                out=var_eps[:], in0=mean_var[:, :, 1], scalar1=EPS, scalar2=1.0, op0=ALU.add, op1=ALU.mult
+            )
+            rstd = small.tile([P, GROUPS], F32, name="rstd")
+            nc.gpsimd.tensor_tensor(out=rstd[:], in0=var_eps[:], in1=minus_half[:], op=ALU.pow)
+            mean_var_of[r], rstd_of[r] = mean_var, rstd
+
+        def normalise(r):
+            x_sb, mean_var, rstd = x_of[r], mean_var_of[r], rstd_of[r]
+            shift = small.tile([P, GROUPS], F32, name="shift")
+            nc.vector.scalar_tensor_tensor(
+                out=shift[:], in0=mean_var[:, :, 0], scalar=-1.0, in1=rstd[:], op0=ALU.mult, op1=ALU.mult
+            )
+            r_sb = r_pool.tile([P, TILES, E], F32, name="r_sb")
+            for j in range(TILES):
+                for h in range(HEADS):
+                    i = j * HEADS + h
+                    cols = slice(h * HEAD, (h + 1) * HEAD)
+                    nc.scalar.activation(
+                        out=r_sb[:, j, cols], in_=x_sb[:, j, cols], func=ACT.Identity,
+                        scale=rstd[:, i : i + 1], bias=shift[:, i : i + 1],
+                    )
+            r_of[r] = r_sb
+
+        def transpose_and_leave_psum(r):
+            r_sb, g_sb = r_of[r], g_of[r]
+            r_banks, g_banks = [], []
+            for c in range(PASSES):
+                g_bank = psum_g.tile([P, PACK, TOK], BF16, name="g_bank")
+                for t in range(PACK):
+                    m = c * PACK + t
+                    for j in range(TILES):
+                        nc.tensor.transpose(
+                            g_bank[:, t, j * P : (j + 1) * P], g_sb[:, j, m * P : (m + 1) * P], ident_bf16[:]
+                        )
+                g_banks.append(g_bank)
+                for half in range(PACK // 2):
+                    r_bank = psum_r.tile([P, 2, TOK], F32, name="r_bank")
+                    for i in range(2):
+                        m = c * PACK + 2 * half + i
+                        for j in range(TILES):
+                            nc.tensor.transpose(
+                                r_bank[:, i, j * P : (j + 1) * P], r_sb[:, j, m * P : (m + 1) * P], ident_f32[:]
+                            )
+                    r_banks.append(r_bank)
+            rn_of[r], silu_of[r] = [], []
+            for c in range(PASSES):
+                silu_t = t_pool.tile([P, PACK, TOK], F32, name="silu_t")
+                nc.scalar.activation(out=silu_t[:], in_=g_banks[c][:], func=ACT.Silu)
+                rn_t = t_pool.tile([P, PACK, TOK], F32, name="rn_t")
+                for t in range(PACK):
+                    m = c * PACK + t
+                    nc.scalar.activation(
+                        out=rn_t[:, t, :], in_=r_banks[m // 2][:, m % 2, :], func=ACT.Identity,
+                        scale=weight_col[:, m : m + 1], bias=bias_col[:, m : m + 1],
+                    )
+                silu_of[r].append(silu_t)
+                rn_of[r].append(rn_t)
+
+        def gate_and_quantise(r):
+            rn_ts, silu_ts = rn_of[r], silu_of[r]
+            gate = q_pool.tile([P, PASSES, TOK, PACK], BF16, name="gate", align_bytes=64)
+            for c in range(PASSES):
+                nc.vector.tensor_tensor(
+                    out=gate[:, c],
+                    in0=rn_ts[c][:].rearrange("p t k -> p k t"),
+                    in1=silu_ts[c][:].rearrange("p t k -> p k t"),
+                    op=ALU.mult,
+                )
+            codes = q_pool.tile([P, PASSES * TOK], U32, name="codes", align_bytes=64)
+            scales = q_pool.tile([P, PASSES * TOK], U8, name="scales", align_bytes=64)
+            nc.vector.quantize_mx(
+                out=codes[:].bitcast(FP8X4), scales=scales[:], in_=gate[:].rearrange("p c k t -> p (c k t)")
+            )
+            codes_of[r], scales_of[r] = codes, scales
+
+        def project_and_store(r):
+            codes, scales = codes_of[r], scales_of[r]
+            out_sb = o_pool.tile([P, TILES, E], F32, name="out_sb")
+            for j in range(TILES):
+                for n in range(N_HALVES):
+                    n_cols = slice(n * N_BANK, (n + 1) * N_BANK)
+                    acc = psum_o.tile([P, N_BANK], F32, name="acc")
+                    for c in range(PASSES):
+                        tokens = slice(c * TOK + j * P, c * TOK + (j + 1) * P)
+                        nc.tensor.matmul_mx(
+                            out=acc[:],
+                            lhsT=codes[:, tokens].bitcast(FP8X4),
+                            lhsT_scale=scales[:, tokens],
+                            rhs=w_codes[:, c, n_cols].bitcast(FP8X4),
+                            rhs_scale=w_scales[:, c, n_cols],
+                            start=(c == 0),
+                            stop=(c == PASSES - 1),
+                        )
+                    nc.vector.tensor_tensor(out=out_sb[:, j, n_cols], in0=acc[:], in1=b_all[:, n_cols], op=ALU.add)
+            nc.sync.dma_start(out=out_rounds[r], in_=out_sb[:])
+
+        load_ret(0)
+
+        ident_f32 = const.tile([P, P], F32, name="ident_f32")
+        make_identity(nc, ident_f32[:])
+        ident_bf16 = const.tile([P, P], BF16, name="ident_bf16")
+        make_identity(nc, ident_bf16[:])
+        minus_half = const.tile([P, GROUPS], F32, name="minus_half")
+        nc.gpsimd.memset(minus_half[:], -0.5)
+
+        rows = const.tile([P, P], BF16, name="rows")
+        nc.vector.memset(rows[:], 0.0)
+        nc.scalar.dma_start(out=rows[0:K_BLOCKS, :], in_=gn_weight.rearrange("(m p) -> m p", p=P))
+        nc.scalar.dma_start(out=rows[K_BLOCKS : 2 * K_BLOCKS, :], in_=gn_bias.rearrange("(m p) -> m p", p=P))
+        cols_bank = psum_g.tile([P, PACK, TOK], BF16, name="g_bank")
+        nc.tensor.transpose(cols_bank[:, 0, 0:P], rows[:], ident_bf16[:])
+        weight_col = const.tile([P, K_BLOCKS], F32, name="weight_col")
+        nc.vector.tensor_copy(out=weight_col[:], in_=cols_bank[:, 0, 0:K_BLOCKS])
+        bias_col = const.tile([P, K_BLOCKS], F32, name="bias_col")
+        nc.vector.tensor_copy(out=bias_col[:], in_=cols_bank[:, 0, K_BLOCKS : 2 * K_BLOCKS])
+
+        b_all = const.tile([P, E], BF16, name="b_all")
+        nc.scalar.dma_start(out=b_all[:], in_=b_o.partition_broadcast(P))
+
+        w_codes = const.tile([P, PASSES, E], U32, name="w_codes", align_bytes=64)
+        w_scales = const.tile([P, PASSES, E], U8, name="w_scales", align_bytes=64)
+        for c in range(PASSES):
+            w_raw = w_stage.tile([P, PACK, E], BF16, name="w_raw")
+            nc.sync.dma_start(out=w_raw[:], in_=w_passes[c])
+            w_grouped = w_stage.tile([P, E, PACK], BF16, name="w_grouped", align_bytes=64)
+            for piece in range(W_PIECES):
+                n_cols = slice(piece * E // W_PIECES, (piece + 1) * E // W_PIECES)
+                nc.gpsimd.tensor_scalar(
+                    out=w_grouped[:, n_cols, :], in0=w_raw[:, :, n_cols].rearrange("p t n -> p n t"),
+                    scalar1=1.0, scalar2=0.0, op0=ALU.mult, op1=ALU.add,
+                )
+            nc.vector.quantize_mx(
+                out=w_codes[:, c, :].bitcast(FP8X4),
+                scales=w_scales[:, c, :],
+                in_=w_grouped[:].rearrange("p n t -> p (n t)"),
+            )
+
+        for step in range(ROUNDS + 4):
+            if step + 1 < ROUNDS:
+                load_ret(step + 1)
+            if step < ROUNDS:
+                load_g(step)
+                statistics(step)
+            if 0 <= step - 1 < ROUNDS:
+                normalise(step - 1)
+            if 0 <= step - 2 < ROUNDS:
+                transpose_and_leave_psum(step - 2)
+            if 0 <= step - 4 < ROUNDS:
+                project_and_store(step - 4)
+            if 0 <= step - 3 < ROUNDS:
+                gate_and_quantise(step - 3)

@@ -73,9 +73,9 @@ def tile_multiscaleretention_pc_t_kernel(tc, ret, g, gn_weight, gn_bias, w_o, b_
             mean_var = small.tile([P, GROUPS, 2], F32, name="mean_var")
             for j in range(TILES):
                 for h in range(HEADS):
-                    i = j * HEADS + h
-                    nc.vector.bn_stats(out=stats[:, i, :], in_=x_sb[:, j, h * HEAD : (h + 1) * HEAD])
-                    nc.vector.bn_aggr(out=mean_var[:, i, :], in_=stats[:, i, :])
+                    nc.vector.bn_stats(out=stats[:, j * HEADS + h, :], in_=x_sb[:, j, h * HEAD : (h + 1) * HEAD])
+            for i in range(GROUPS):
+                nc.vector.bn_aggr(out=mean_var[:, i, :], in_=stats[:, i, :])
             var_eps = small.tile([P, GROUPS], F32, name="var_eps")
             nc.gpsimd.tensor_scalar(
                 out=var_eps[:], in0=mean_var[:, :, 1], scalar1=EPS, scalar2=1.0, op0=ALU.add, op1=ALU.mult

@@ -27,6 +27,7 @@ ROUNDS = TOKENS // TOK
 GROUPS = TILES * HEADS
 N_BANK = 512
 N_HALVES = E // N_BANK
+RUN = 4
 W_PIECES = 4
 
 FLOPS = 2 * TOKENS * E * E
@@ -141,9 +142,9 @@ def tile_multiscaleretention_pc_t_kernel(tc, ret, g, gn_weight, gn_bias, w_o, b_
             gate = q_pool.tile([P, PASSES, TOK, PACK], BF16, name="gate", align_bytes=64)
             for c in range(PASSES):
                 nc.vector.tensor_tensor(
-                    out=gate[:, c],
-                    in0=rn_ts[c][:].rearrange("p t k -> p k t"),
-                    in1=silu_ts[c][:].rearrange("p t k -> p k t"),
+                    out=gate[:, c].rearrange("p (q i) t -> p q t i", i=RUN),
+                    in0=rn_ts[c][:].rearrange("p t (q i) -> p q t i", i=RUN),
+                    in1=silu_ts[c][:].rearrange("p t (q i) -> p q t i", i=RUN),
                     op=ALU.mult,
                 )
             codes = q_pool.tile([P, PASSES * TOK], U32, name="codes", align_bytes=64)

@@ -28,7 +28,6 @@ GROUPS = TILES * HEADS
 N_BANK = 512
 N_HALVES = E // N_BANK
 RUN = 4
-W_PIECES = 4
 
 FLOPS = 2 * TOKENS * E * E
 
@@ -53,10 +52,12 @@ def tile_multiscaleretention_pc_t_kernel(tc, ret, g, gn_weight, gn_bias, w_o, b_
         psum_r = ctx.enter_context(tc.psum_pool(name="psum_r", bufs=4))
         psum_g = ctx.enter_context(tc.psum_pool(name="psum_g", bufs=2))
         psum_o = ctx.enter_context(tc.psum_pool(name="psum_o", bufs=2))
+        ctx.enter_context(tc.manual_schedule())
 
-        x_of, g_of, mean_var_of, rstd_of, r_of, rn_of, silu_of, codes_of, scales_of = (
-            {}, {}, {}, {}, {}, {}, {}, {}, {},
+        x_of, g_of, mean_var_of, rstd_of, shift_of, r_of, rn_of, silu_of, planes_of, codes_of, scales_of = (
+            {}, {}, {}, {}, {}, {}, {}, {}, {}, {}, {},
         )
+        w_raw_of, w_grouped_of = {}, {}
 
         def load_ret(r):
             x_sb = x_pool.tile([P, TILES, E], BF16, name="x_sb")
@@ -68,7 +69,7 @@ def tile_multiscaleretention_pc_t_kernel(tc, ret, g, gn_weight, gn_bias, w_o, b_
             nc.sync.dma_start(out=g_sb[:], in_=g_rounds[r])
             g_of[r] = g_sb
 
-        def statistics(r):
+        def mean_and_variance(r):
             x_sb = x_of[r]
             stats = small.tile([P, GROUPS, 6], F32, name="stats")
             mean_var = small.tile([P, GROUPS, 2], F32, name="mean_var")
@@ -77,20 +78,26 @@ def tile_multiscaleretention_pc_t_kernel(tc, ret, g, gn_weight, gn_bias, w_o, b_
                     nc.vector.bn_stats(out=stats[:, j * HEADS + h, :], in_=x_sb[:, j, h * HEAD : (h + 1) * HEAD])
             for i in range(GROUPS):
                 nc.vector.bn_aggr(out=mean_var[:, i, :], in_=stats[:, i, :])
+            mean_var_of[r] = mean_var
+
+        def reciprocal_std(r):
             var_eps = small.tile([P, GROUPS], F32, name="var_eps")
             nc.gpsimd.tensor_scalar(
-                out=var_eps[:], in0=mean_var[:, :, 1], scalar1=EPS, scalar2=1.0, op0=ALU.add, op1=ALU.mult
+                out=var_eps[:], in0=mean_var_of[r][:, :, 1], scalar1=EPS, scalar2=1.0, op0=ALU.add, op1=ALU.mult
             )
             rstd = small.tile([P, GROUPS], F32, name="rstd")
             nc.gpsimd.tensor_tensor(out=rstd[:], in0=var_eps[:], in1=minus_half[:], op=ALU.pow)
-            mean_var_of[r], rstd_of[r] = mean_var, rstd
+            rstd_of[r] = rstd
 
-        def normalise(r):
-            x_sb, mean_var, rstd = x_of[r], mean_var_of[r], rstd_of[r]
+        def shift_of_mean(r):
             shift = small.tile([P, GROUPS], F32, name="shift")
             nc.vector.scalar_tensor_tensor(
-                out=shift[:], in0=mean_var[:, :, 0], scalar=-1.0, in1=rstd[:], op0=ALU.mult, op1=ALU.mult
+                out=shift[:], in0=mean_var_of[r][:, :, 0], scalar=-1.0, in1=rstd_of[r][:], op0=ALU.mult, op1=ALU.mult
             )
+            shift_of[r] = shift
+
+        def normalise(r):
+            x_sb, rstd, shift = x_of[r], rstd_of[r], shift_of[r]
             r_sb = r_pool.tile([P, TILES, E], F32, name="r_sb")
             for j in range(TILES):
                 for h in range(HEADS):
@@ -137,36 +144,42 @@ def tile_multiscaleretention_pc_t_kernel(tc, ret, g, gn_weight, gn_bias, w_o, b_
                 silu_of[r].append(silu_t)
                 rn_of[r].append(rn_t)
 
-        def gate_and_quantise(r):
-            rn_ts, silu_ts = rn_of[r], silu_of[r]
-            gate = q_pool.tile([P, PASSES, TOK, PACK], BF16, name="gate", align_bytes=64)
+        def product(r):
+            planes = q_pool.tile([P, PASSES, PACK, TOK], BF16, name="planes")
             for c in range(PASSES):
-                nc.vector.tensor_tensor(
+                nc.gpsimd.tensor_tensor(out=planes[:, c], in0=rn_of[r][c][:], in1=silu_of[r][c][:], op=ALU.mult)
+            planes_of[r] = planes
+
+        def quantise(r):
+            planes = planes_of[r]
+            gate = q_pool.tile([P, PASSES, TOK, PACK], BF16, name="gate", align_bytes=64)
+            codes = q_pool.tile([P, PASSES, TOK], U32, name="codes", align_bytes=64)
+            scales = q_pool.tile([P, PASSES, TOK], U8, name="scales", align_bytes=64)
+            for c in range(PASSES):
+                nc.vector.tensor_copy(
                     out=gate[:, c].rearrange("p (q i) t -> p q t i", i=RUN),
-                    in0=rn_ts[c][:].rearrange("p t (q i) -> p q t i", i=RUN),
-                    in1=silu_ts[c][:].rearrange("p t (q i) -> p q t i", i=RUN),
-                    op=ALU.mult,
+                    in_=planes[:, c].rearrange("p t (q i) -> p q t i", i=RUN),
                 )
-            codes = q_pool.tile([P, PASSES * TOK], U32, name="codes", align_bytes=64)
-            scales = q_pool.tile([P, PASSES * TOK], U8, name="scales", align_bytes=64)
-            nc.vector.quantize_mx(
-                out=codes[:].bitcast(FP8X4), scales=scales[:], in_=gate[:].rearrange("p c k t -> p (c k t)")
-            )
+            for c in range(PASSES):
+                nc.vector.quantize_mx(
+                    out=codes[:, c, :].bitcast(FP8X4), scales=scales[:, c, :],
+                    in_=gate[:, c].rearrange("p k t -> p (k t)"),
+                )
             codes_of[r], scales_of[r] = codes, scales
 
         def project_and_store(r):
             codes, scales = codes_of[r], scales_of[r]
             out_sb = o_pool.tile([P, TILES, E], F32, name="out_sb")
             for j in range(TILES):
+                tokens = slice(j * P, (j + 1) * P)
                 for n in range(N_HALVES):
                     n_cols = slice(n * N_BANK, (n + 1) * N_BANK)
                     acc = psum_o.tile([P, N_BANK], F32, name="acc")
                     for c in range(PASSES):
-                        tokens = slice(c * TOK + j * P, c * TOK + (j + 1) * P)
                         nc.tensor.matmul_mx(
                             out=acc[:],
-                            lhsT=codes[:, tokens].bitcast(FP8X4),
-                            lhsT_scale=scales[:, tokens],
+                            lhsT=codes[:, c, tokens].bitcast(FP8X4),
+                            lhsT_scale=scales[:, c, tokens],
                             rhs=w_codes[:, c, n_cols].bitcast(FP8X4),
                             rhs_scale=w_scales[:, c, n_cols],
                             start=(c == 0),
@@ -174,6 +187,26 @@ def tile_multiscaleretention_pc_t_kernel(tc, ret, g, gn_weight, gn_bias, w_o, b_
                         )
                     nc.vector.tensor_tensor(out=out_sb[:, j, n_cols], in0=acc[:], in1=b_all[:, n_cols], op=ALU.add)
             nc.sync.dma_start(out=out_rounds[r], in_=out_sb[:])
+
+        def load_w(c):
+            w_raw = w_stage.tile([P, PACK, E], BF16, name="w_raw")
+            nc.sync.dma_start(out=w_raw[:], in_=w_passes[c])
+            w_raw_of[c] = w_raw
+
+        def regroup_w(c):
+            w_grouped = w_stage.tile([P, E, PACK], BF16, name="w_grouped", align_bytes=64)
+            nc.vector.tensor_copy(
+                out=w_grouped[:].rearrange("p (q i) t -> p q t i", i=RUN),
+                in_=w_raw_of[c][:].rearrange("p t (q i) -> p q t i", i=RUN),
+            )
+            w_grouped_of[c] = w_grouped
+
+        def quantise_w(c):
+            nc.vector.quantize_mx(
+                out=w_codes[:, c, :].bitcast(FP8X4),
+                scales=w_scales[:, c, :],
+                in_=w_grouped_of[c][:].rearrange("p n t -> p (n t)"),
+            )
 
         load_ret(0)
 
@@ -183,6 +216,8 @@ def tile_multiscaleretention_pc_t_kernel(tc, ret, g, gn_weight, gn_bias, w_o, b_
         make_identity(nc, ident_bf16[:])
         minus_half = const.tile([P, GROUPS], F32, name="minus_half")
         nc.gpsimd.memset(minus_half[:], -0.5)
+        w_codes = const.tile([P, PASSES, E], U32, name="w_codes", align_bytes=64)
+        w_scales = const.tile([P, PASSES, E], U8, name="w_scales", align_bytes=64)
 
         rows = const.tile([P, P], BF16, name="rows")
         nc.vector.memset(rows[:], 0.0)
@@ -191,42 +226,38 @@ def tile_multiscaleretention_pc_t_kernel(tc, ret, g, gn_weight, gn_bias, w_o, b_
         cols_bank = psum_g.tile([P, PACK, TOK], BF16, name="g_bank")
         nc.tensor.transpose(cols_bank[:, 0, 0:P], rows[:], ident_bf16[:])
         weight_col = const.tile([P, K_BLOCKS], F32, name="weight_col")
-        nc.vector.tensor_copy(out=weight_col[:], in_=cols_bank[:, 0, 0:K_BLOCKS])
         bias_col = const.tile([P, K_BLOCKS], F32, name="bias_col")
-        nc.vector.tensor_copy(out=bias_col[:], in_=cols_bank[:, 0, K_BLOCKS : 2 * K_BLOCKS])
 
         b_all = const.tile([P, E], BF16, name="b_all")
         nc.scalar.dma_start(out=b_all[:], in_=b_o.partition_broadcast(P))
 
-        w_codes = const.tile([P, PASSES, E], U32, name="w_codes", align_bytes=64)
-        w_scales = const.tile([P, PASSES, E], U8, name="w_scales", align_bytes=64)
-        for c in range(PASSES):
-            w_raw = w_stage.tile([P, PACK, E], BF16, name="w_raw")
-            nc.sync.dma_start(out=w_raw[:], in_=w_passes[c])
-            w_grouped = w_stage.tile([P, E, PACK], BF16, name="w_grouped", align_bytes=64)
-            for piece in range(W_PIECES):
-                n_cols = slice(piece * E // W_PIECES, (piece + 1) * E // W_PIECES)
-                nc.gpsimd.tensor_scalar(
-                    out=w_grouped[:, n_cols, :], in0=w_raw[:, :, n_cols].rearrange("p t n -> p n t"),
-                    scalar1=1.0, scalar2=0.0, op0=ALU.mult, op1=ALU.add,
-                )
-            nc.vector.quantize_mx(
-                out=w_codes[:, c, :].bitcast(FP8X4),
-                scales=w_scales[:, c, :],
-                in_=w_grouped[:].rearrange("p n t -> p (n t)"),
-            )
-
-        for step in range(ROUNDS + 4):
+        for step in range(ROUNDS + 5):
             if step + 1 < ROUNDS:
                 load_ret(step + 1)
             if step < ROUNDS:
                 load_g(step)
-                statistics(step)
+            if 0 <= step - 1 < PASSES:
+                load_w(step - 1)
+            if 0 <= step - 1 < ROUNDS:
+                shift_of_mean(step - 1)
+            if step < ROUNDS:
+                mean_and_variance(step)
+            if step == 0:
+                nc.vector.tensor_copy(out=weight_col[:], in_=cols_bank[:, 0, 0:K_BLOCKS])
+                nc.vector.tensor_copy(out=bias_col[:], in_=cols_bank[:, 0, K_BLOCKS : 2 * K_BLOCKS])
+            if 0 <= step - 3 < ROUNDS:
+                product(step - 3)
+            if step < ROUNDS:
+                reciprocal_std(step)
             if 0 <= step - 1 < ROUNDS:
                 normalise(step - 1)
             if 0 <= step - 2 < ROUNDS:
                 transpose_and_leave_psum(step - 2)
+            if 0 <= step - 5 < ROUNDS:
+                project_and_store(step - 5)
             if 0 <= step - 4 < ROUNDS:
-                project_and_store(step - 4)
-            if 0 <= step - 3 < ROUNDS:
-                gate_and_quantise(step - 3)
+                quantise(step - 4)
+            if 0 <= step - 3 < PASSES:
+                quantise_w(step - 3)
+            if 0 <= step - 2 < PASSES:
+                regroup_w(step - 2)

@@ -28,6 +28,7 @@ GROUPS = TILES * HEADS
 N_BANK = 512
 N_HALVES = E // N_BANK
 RUN = 4
+AHEAD = 3
 
 FLOPS = 2 * TOKENS * E * E
 
@@ -42,11 +43,11 @@ def tile_multiscaleretention_pc_t_kernel(tc, ret, g, gn_weight, gn_bias, w_o, b_
     with ExitStack() as ctx:
         const = ctx.enter_context(tc.tile_pool(name="const", bufs=1))
         w_stage = ctx.enter_context(tc.tile_pool(name="w_stage", bufs=2))
-        x_pool = ctx.enter_context(tc.tile_pool(name="x", bufs=4))
+        x_pool = ctx.enter_context(tc.tile_pool(name="x", bufs=AHEAD + 3))
         g_pool = ctx.enter_context(tc.tile_pool(name="g", bufs=4))
-        small = ctx.enter_context(tc.tile_pool(name="small", bufs=4))
+        small = ctx.enter_context(tc.tile_pool(name="small", bufs=AHEAD + 2))
         r_pool = ctx.enter_context(tc.tile_pool(name="r", bufs=3))
-        t_pool = ctx.enter_context(tc.tile_pool(name="transposed", bufs=5))
+        t_pool = ctx.enter_context(tc.tile_pool(name="transposed", bufs=4))
         q_pool = ctx.enter_context(tc.tile_pool(name="quantised", bufs=3))
         o_pool = ctx.enter_context(tc.tile_pool(name="o", bufs=3))
         psum_r = ctx.enter_context(tc.psum_pool(name="psum_r", bufs=4))
@@ -54,152 +55,145 @@ def tile_multiscaleretention_pc_t_kernel(tc, ret, g, gn_weight, gn_bias, w_o, b_
         psum_o = ctx.enter_context(tc.psum_pool(name="psum_o", bufs=2))
         ctx.enter_context(tc.manual_schedule())
 
-        x_of, g_of, mean_var_of, rstd_of, shift_of, r_of, rn_of, silu_of, planes_of, codes_of, scales_of = (
-            {}, {}, {}, {}, {}, {}, {}, {}, {}, {}, {},
+        x_of, g_of, stats_of, rstd_of, shift_of, r_of, gate_of, codes_of, scales_of, out_of = (
+            {}, {}, {}, {}, {}, {}, {}, {}, {}, {},
         )
+        g_bank_of, r_banks_of, silu_of, rn_of, acc_of = {}, {}, {}, {}, {}
         w_raw_of, w_grouped_of = {}, {}
 
         def load_ret(r):
-            x_sb = x_pool.tile([P, TILES, E], BF16, name="x_sb")
-            nc.sync.dma_start(out=x_sb[:], in_=ret_rounds[r])
-            x_of[r] = x_sb
+            x_of[r] = x_pool.tile([P, TILES, E], BF16, name="x_sb")
+            nc.sync.dma_start(out=x_of[r][:], in_=ret_rounds[r])
 
         def load_g(r):
-            g_sb = g_pool.tile([P, TILES, E], BF16, name="g_sb")
-            nc.sync.dma_start(out=g_sb[:], in_=g_rounds[r])
-            g_of[r] = g_sb
+            g_of[r] = g_pool.tile([P, TILES, E], BF16, name="g_sb")
+            nc.sync.dma_start(out=g_of[r][:], in_=g_rounds[r])
 
-        def mean_and_variance(r):
-            x_sb = x_of[r]
-            stats = small.tile([P, GROUPS, 6], F32, name="stats")
-            mean_var = small.tile([P, GROUPS, 2], F32, name="mean_var")
+        def statistics(r):
+            stats = small.tile([P, GROUPS, 3], F32, name="stats")
             for j in range(TILES):
-                for h in range(HEADS):
-                    nc.vector.bn_stats(out=stats[:, j * HEADS + h, :], in_=x_sb[:, j, h * HEAD : (h + 1) * HEAD])
-            for i in range(GROUPS):
-                nc.vector.bn_aggr(out=mean_var[:, i, :], in_=stats[:, i, :])
-            mean_var_of[r] = mean_var
+                for pair in range(HEADS // 2):
+                    i = j * HEADS + 2 * pair
+                    nc.vector.bn_stats(
+                        out=stats[:, i : i + 2, :].rearrange("p a s -> p (a s)"),
+                        in_=x_of[r][:, j, 2 * pair * HEAD : 2 * (pair + 1) * HEAD].rearrange("p (a d) -> p d a", a=2),
+                    )
+            stats_of[r] = stats
 
-        def reciprocal_std(r):
+        def scale_and_shift(r):
+            mean, count_var = stats_of[r][:, :, 1], stats_of[r][:, :, 2]
             var_eps = small.tile([P, GROUPS], F32, name="var_eps")
             nc.gpsimd.tensor_scalar(
-                out=var_eps[:], in0=mean_var_of[r][:, :, 1], scalar1=EPS, scalar2=1.0, op0=ALU.add, op1=ALU.mult
+                out=var_eps[:], in0=count_var, scalar1=1.0 / HEAD, scalar2=EPS, op0=ALU.mult, op1=ALU.add
             )
-            rstd = small.tile([P, GROUPS], F32, name="rstd")
-            nc.gpsimd.tensor_tensor(out=rstd[:], in0=var_eps[:], in1=minus_half[:], op=ALU.pow)
-            rstd_of[r] = rstd
-
-        def shift_of_mean(r):
-            shift = small.tile([P, GROUPS], F32, name="shift")
-            nc.vector.scalar_tensor_tensor(
-                out=shift[:], in0=mean_var_of[r][:, :, 0], scalar=-1.0, in1=rstd_of[r][:], op0=ALU.mult, op1=ALU.mult
-            )
-            shift_of[r] = shift
+            minus_mean = small.tile([P, GROUPS], F32, name="minus_mean")
+            nc.gpsimd.tensor_scalar(out=minus_mean[:], in0=mean, scalar1=-1.0, scalar2=0.0, op0=ALU.mult, op1=ALU.add)
+            rstd_of[r] = small.tile([P, GROUPS], F32, name="rstd")
+            nc.gpsimd.tensor_tensor(out=rstd_of[r][:], in0=var_eps[:], in1=minus_half[:], op=ALU.pow)
+            shift_of[r] = small.tile([P, GROUPS], F32, name="shift")
+            nc.gpsimd.tensor_tensor(out=shift_of[r][:], in0=minus_mean[:], in1=rstd_of[r][:], op=ALU.mult)
 
         def normalise(r):
-            x_sb, rstd, shift = x_of[r], rstd_of[r], shift_of[r]
-            r_sb = r_pool.tile([P, TILES, E], F32, name="r_sb")
+            r_of[r] = r_pool.tile([P, TILES, E], F32, name="r_sb")
             for j in range(TILES):
                 for h in range(HEADS):
                     i = j * HEADS + h
                     cols = slice(h * HEAD, (h + 1) * HEAD)
                     nc.scalar.activation(
-                        out=r_sb[:, j, cols], in_=x_sb[:, j, cols], func=ACT.Identity,
-                        scale=rstd[:, i : i + 1], bias=shift[:, i : i + 1],
+                        out=r_of[r][:, j, cols], in_=x_of[r][:, j, cols], func=ACT.Identity,
+                        scale=rstd_of[r][:, i : i + 1], bias=shift_of[r][:, i : i + 1],
                     )
-            r_of[r] = r_sb
 
-        def transpose_and_leave_psum(r):
-            r_sb, g_sb = r_of[r], g_of[r]
-            r_banks, g_banks = [], []
-            for c in range(PASSES):
-                g_bank = psum_g.tile([P, PACK, TOK], BF16, name="g_bank")
-                for t in range(PACK):
-                    m = c * PACK + t
+        def transpose_g(r, c):
+            g_bank = psum_g.tile([P, PACK, TOK], BF16, name="g_bank")
+            for t in range(PACK):
+                m = c * PACK + t
+                for j in range(TILES):
+                    nc.tensor.transpose(
+                        g_bank[:, t, j * P : (j + 1) * P], g_of[r][:, j, m * P : (m + 1) * P], ident_bf16[:]
+                    )
+            g_bank_of[r, c] = g_bank
+
+        def transpose_r(r, c):
+            r_banks_of[r, c] = []
+            for half in range(PACK // 2):
+                r_bank = psum_r.tile([P, 2, TOK], F32, name="r_bank")
+                for i in range(2):
+                    m = c * PACK + 2 * half + i
                     for j in range(TILES):
                         nc.tensor.transpose(
-                            g_bank[:, t, j * P : (j + 1) * P], g_sb[:, j, m * P : (m + 1) * P], ident_bf16[:]
+                            r_bank[:, i, j * P : (j + 1) * P], r_of[r][:, j, m * P : (m + 1) * P], ident_f32[:]
                         )
-                g_banks.append(g_bank)
-                for half in range(PACK // 2):
-                    r_bank = psum_r.tile([P, 2, TOK], F32, name="r_bank")
-                    for i in range(2):
-                        m = c * PACK + 2 * half + i
-                        for j in range(TILES):
-                            nc.tensor.transpose(
-                                r_bank[:, i, j * P : (j + 1) * P], r_sb[:, j, m * P : (m + 1) * P], ident_f32[:]
-                            )
-                    r_banks.append(r_bank)
-            rn_of[r], silu_of[r] = [], []
-            for c in range(PASSES):
-                silu_t = t_pool.tile([P, PACK, TOK], F32, name="silu_t")
-                nc.scalar.activation(out=silu_t[:], in_=g_banks[c][:], func=ACT.Silu)
-                rn_t = t_pool.tile([P, PACK, TOK], F32, name="rn_t")
-                for t in range(PACK):
-                    m = c * PACK + t
-                    nc.scalar.activation(
-                        out=rn_t[:, t, :], in_=r_banks[m // 2][:, m % 2, :], func=ACT.Identity,
-                        scale=weight_col[:, m : m + 1], bias=bias_col[:, m : m + 1],
-                    )
-                silu_of[r].append(silu_t)
-                rn_of[r].append(rn_t)
+                r_banks_of[r, c].append(r_bank)
 
-        def product(r):
-            planes = q_pool.tile([P, PASSES, PACK, TOK], BF16, name="planes")
-            for c in range(PASSES):
-                nc.gpsimd.tensor_tensor(out=planes[:, c], in0=rn_of[r][c][:], in1=silu_of[r][c][:], op=ALU.mult)
-            planes_of[r] = planes
+        def leave_psum(r, c):
+            silu_of[r, c] = t_pool.tile([P, PACK, TOK], F32, name="silu_t")
+            nc.scalar.activation(out=silu_of[r, c][:], in_=g_bank_of[r, c][:], func=ACT.Silu)
+            rn_of[r, c] = t_pool.tile([P, PACK, TOK], F32, name="rn_t")
+            for t in range(PACK):
+                m = c * PACK + t
+                nc.scalar.activation(
+                    out=rn_of[r, c][:, t, :], in_=r_banks_of[r, c][t // 2][:, t % 2, :], func=ACT.Identity,
+                    scale=weight_col[:, m : m + 1], bias=bias_col[:, m : m + 1],
+                )
+
+        def product(r, c):
+            if c == 0:
+                gate_of[r] = q_pool.tile([P, PASSES, TOK, PACK], BF16, name="gate", align_bytes=64)
+            nc.vector.tensor_tensor(
+                out=gate_of[r][:, c].rearrange("p (q i) t -> p q t i", i=RUN),
+                in0=rn_of[r, c][:].rearrange("p t (q i) -> p q t i", i=RUN),
+                in1=silu_of[r, c][:].rearrange("p t (q i) -> p q t i", i=RUN),
+                op=ALU.mult,
+            )
 
         def quantise(r):
-            planes = planes_of[r]
-            gate = q_pool.tile([P, PASSES, TOK, PACK], BF16, name="gate", align_bytes=64)
-            codes = q_pool.tile([P, PASSES, TOK], U32, name="codes", align_bytes=64)
-            scales = q_pool.tile([P, PASSES, TOK], U8, name="scales", align_bytes=64)
-            for c in range(PASSES):
-                nc.vector.tensor_copy(
-                    out=gate[:, c].rearrange("p (q i) t -> p q t i", i=RUN),
-                    in_=planes[:, c].rearrange("p t (q i) -> p q t i", i=RUN),
-                )
-            for c in range(PASSES):
-                nc.vector.quantize_mx(
-                    out=codes[:, c, :].bitcast(FP8X4), scales=scales[:, c, :],
-                    in_=gate[:, c].rearrange("p k t -> p (k t)"),
-                )
-            codes_of[r], scales_of[r] = codes, scales
+            codes_of[r] = q_pool.tile([P, PASSES, TOK], U32, name="codes", align_bytes=64)
+            scales_of[r] = q_pool.tile([P, PASSES, TOK], U8, name="scales", align_bytes=64)
+            nc.vector.quantize_mx(
+                out=codes_of[r][:].rearrange("p c k -> p (c k)").bitcast(FP8X4),
+                scales=scales_of[r][:].rearrange("p c k -> p (c k)"),
+                in_=gate_of[r][:].rearrange("p c k t -> p (c k t)"),
+            )
 
-        def project_and_store(r):
-            codes, scales = codes_of[r], scales_of[r]
-            out_sb = o_pool.tile([P, TILES, E], F32, name="out_sb")
-            for j in range(TILES):
-                tokens = slice(j * P, (j + 1) * P)
-                for n in range(N_HALVES):
-                    n_cols = slice(n * N_BANK, (n + 1) * N_BANK)
-                    acc = psum_o.tile([P, N_BANK], F32, name="acc")
-                    for c in range(PASSES):
-                        nc.tensor.matmul_mx(
-                            out=acc[:],
-                            lhsT=codes[:, c, tokens].bitcast(FP8X4),
-                            lhsT_scale=scales[:, c, tokens],
-                            rhs=w_codes[:, c, n_cols].bitcast(FP8X4),
-                            rhs_scale=w_scales[:, c, n_cols],
-                            start=(c == 0),
-                            stop=(c == PASSES - 1),
-                        )
-                    nc.vector.tensor_tensor(out=out_sb[:, j, n_cols], in0=acc[:], in1=b_all[:, n_cols], op=ALU.add)
-            nc.sync.dma_start(out=out_rounds[r], in_=out_sb[:])
+        def matmuls(r, j):
+            tokens = slice(j * P, (j + 1) * P)
+            for n in range(N_HALVES):
+                n_cols = slice(n * N_BANK, (n + 1) * N_BANK)
+                acc_of[r, j, n] = psum_o.tile([P, N_BANK], F32, name="acc")
+                for c in range(PASSES):
+                    nc.tensor.matmul_mx(
+                        out=acc_of[r, j, n][:],
+                        lhsT=codes_of[r][:, c, tokens].bitcast(FP8X4),
+                        lhsT_scale=scales_of[r][:, c, tokens],
+                        rhs=w_codes[:, c, n_cols].bitcast(FP8X4),
+                        rhs_scale=w_scales[:, c, n_cols],
+                        start=(c == 0),
+                        stop=(c == PASSES - 1),
+                    )
+
+        def add_bias(r, j):
+            if j == 0:
+                out_of[r] = o_pool.tile([P, TILES, E], F32, name="out_sb")
+            for n in range(N_HALVES):
+                n_cols = slice(n * N_BANK, (n + 1) * N_BANK)
+                nc.vector.tensor_tensor(
+                    out=out_of[r][:, j, n_cols], in0=acc_of[r, j, n][:], in1=b_all[:, n_cols], op=ALU.add
+                )
+
+        def store(r):
+            nc.sync.dma_start(out=out_rounds[r], in_=out_of[r][:])
 
         def load_w(c):
-            w_raw = w_stage.tile([P, PACK, E], BF16, name="w_raw")
-            nc.sync.dma_start(out=w_raw[:], in_=w_passes[c])
-            w_raw_of[c] = w_raw
+            w_raw_of[c] = w_stage.tile([P, PACK, E], BF16, name="w_raw")
+            nc.sync.dma_start(out=w_raw_of[c][:], in_=w_passes[c])
 
         def regroup_w(c):
-            w_grouped = w_stage.tile([P, E, PACK], BF16, name="w_grouped", align_bytes=64)
+            w_grouped_of[c] = w_stage.tile([P, E, PACK], BF16, name="w_grouped", align_bytes=64)
             nc.vector.tensor_copy(
-                out=w_grouped[:].rearrange("p (q i) t -> p q t i", i=RUN),
+                out=w_grouped_of[c][:].rearrange("p (q i) t -> p q t i", i=RUN),
                 in_=w_raw_of[c][:].rearrange("p t (q i) -> p q t i", i=RUN),
             )
-            w_grouped_of[c] = w_grouped
 
         def quantise_w(c):
             nc.vector.quantize_mx(
@@ -207,8 +201,6 @@ def tile_multiscaleretention_pc_t_kernel(tc, ret, g, gn_weight, gn_bias, w_o, b_
                 scales=w_scales[:, c, :],
                 in_=w_grouped_of[c][:].rearrange("p n t -> p (n t)"),
             )
-
-        load_ret(0)
 
         ident_f32 = const.tile([P, P], F32, name="ident_f32")
         make_identity(nc, ident_f32[:])
@@ -231,33 +223,50 @@ def tile_multiscaleretention_pc_t_kernel(tc, ret, g, gn_weight, gn_bias, w_o, b_
         b_all = const.tile([P, E], BF16, name="b_all")
         nc.scalar.dma_start(out=b_all[:], in_=b_o.partition_broadcast(P))
 
-        for step in range(ROUNDS + 5):
-            if step + 1 < ROUNDS:
-                load_ret(step + 1)
-            if step < ROUNDS:
-                load_g(step)
-            if 0 <= step - 1 < PASSES:
-                load_w(step - 1)
-            if 0 <= step - 1 < ROUNDS:
-                shift_of_mean(step - 1)
-            if step < ROUNDS:
-                mean_and_variance(step)
-            if step == 0:
+        def live(r):
+            return 0 <= r < ROUNDS
+
+        first_step = -(AHEAD + 2)
+        for step in range(first_step, ROUNDS + 2):
+            if live(step + AHEAD + 2):
+                load_ret(step + AHEAD + 2)
+            if live(step + 2):
+                load_g(step + 2)
+            if 0 <= step - first_step - 2 < PASSES:
+                load_w(step - first_step - 2)
+
+            if live(step):
+                transpose_r(step, 1)
+            if live(step - 2):
+                matmuls(step - 2, 0)
+                add_bias(step - 2, 0)
+                matmuls(step - 2, 1)
+            if live(step - 1):
+                product(step - 1, 1)
+            if live(step - 2):
+                add_bias(step - 2, 1)
+                store(step - 2)
+            if live(step - 1):
+                quantise(step - 1)
+            if live(step + AHEAD):
+                statistics(step + AHEAD)
+                scale_and_shift(step + AHEAD)
+            if step == -AHEAD:
                 nc.vector.tensor_copy(out=weight_col[:], in_=cols_bank[:, 0, 0:K_BLOCKS])
                 nc.vector.tensor_copy(out=bias_col[:], in_=cols_bank[:, 0, K_BLOCKS : 2 * K_BLOCKS])
-            if 0 <= step - 3 < ROUNDS:
-                product(step - 3)
-            if step < ROUNDS:
-                reciprocal_std(step)
-            if 0 <= step - 1 < ROUNDS:
-                normalise(step - 1)
-            if 0 <= step - 2 < ROUNDS:
-                transpose_and_leave_psum(step - 2)
-            if 0 <= step - 5 < ROUNDS:
-                project_and_store(step - 5)
-            if 0 <= step - 4 < ROUNDS:
-                quantise(step - 4)
-            if 0 <= step - 3 < PASSES:
-                quantise_w(step - 3)
-            if 0 <= step - 2 < PASSES:
-                regroup_w(step - 2)
+            if 0 <= step + 1 < PASSES:
+                quantise_w(step + 1)
+            if 0 <= step + 2 < PASSES:
+                regroup_w(step + 2)
+
+            if live(step + 1):
+                transpose_g(step + 1, 0)
+                transpose_g(step + 1, 1)
+                normalise(step + 1)
+            if live(step):
+                leave_psum(step, 0)
+            if live(step + 1):
+                transpose_r(step + 1, 0)
+            if live(step):
+                product(step, 0)
+                leave_psum(step, 1)

@@ -28,6 +28,7 @@ GROUPS = TILES * HEADS
 N_BANK = 512
 N_HALVES = E // N_BANK
 RUN = 4
+PAIR = 2
 AHEAD = 3
 
 FLOPS = 2 * TOKENS * E * E
@@ -141,9 +142,9 @@ def tile_multiscaleretention_pc_t_kernel(tc, ret, g, gn_weight, gn_bias, w_o, b_
             if c == 0:
                 gate_of[r] = q_pool.tile([P, PASSES, TOK, PACK], BF16, name="gate", align_bytes=64)
             nc.vector.tensor_tensor(
-                out=gate_of[r][:, c].rearrange("p (q i) t -> p q t i", i=RUN),
-                in0=rn_of[r, c][:].rearrange("p t (q i) -> p q t i", i=RUN),
-                in1=silu_of[r, c][:].rearrange("p t (q i) -> p q t i", i=RUN),
+                out=gate_of[r][:, c].rearrange("p (q i) t -> p q t i", i=PAIR),
+                in0=rn_of[r, c][:].rearrange("p t (q i) -> p q t i", i=PAIR),
+                in1=silu_of[r, c][:].rearrange("p t (q i) -> p q t i", i=PAIR),
                 op=ALU.mult,
             )
 

@@ -28,7 +28,7 @@ GROUPS = TILES * HEADS
 N_BANK = 512
 N_HALVES = E // N_BANK
 RUN = 4
-PAIR = 2
+SCALAR_HEADS = 3
 AHEAD = 3
 
 FLOPS = 2 * TOKENS * E * E
@@ -94,10 +94,21 @@ def tile_multiscaleretention_pc_t_kernel(tc, ret, g, gn_weight, gn_bias, w_o, b_
             shift_of[r] = small.tile([P, GROUPS], F32, name="shift")
             nc.gpsimd.tensor_tensor(out=shift_of[r][:], in0=minus_mean[:], in1=rstd_of[r][:], op=ALU.mult)
 
-        def normalise(r):
+        def normalise_on_vector(r):
             r_of[r] = r_pool.tile([P, TILES, E], F32, name="r_sb")
             for j in range(TILES):
-                for h in range(HEADS):
+                for h in range(SCALAR_HEADS, HEADS):
+                    i = j * HEADS + h
+                    cols = slice(h * HEAD, (h + 1) * HEAD)
+                    nc.vector.tensor_scalar(
+                        out=r_of[r][:, j, cols], in0=x_of[r][:, j, cols],
+                        scalar1=stats_of[r][:, i, 1:2], scalar2=rstd_of[r][:, i : i + 1],
+                        op0=ALU.subtract, op1=ALU.mult,
+                    )
+
+        def normalise_on_scalar(r):
+            for j in range(TILES):
+                for h in range(SCALAR_HEADS):
                     i = j * HEADS + h
                     cols = slice(h * HEAD, (h + 1) * HEAD)
                     nc.scalar.activation(
@@ -142,9 +153,9 @@ def tile_multiscaleretention_pc_t_kernel(tc, ret, g, gn_weight, gn_bias, w_o, b_
             if c == 0:
                 gate_of[r] = q_pool.tile([P, PASSES, TOK, PACK], BF16, name="gate", align_bytes=64)
             nc.vector.tensor_tensor(
-                out=gate_of[r][:, c].rearrange("p (q i) t -> p q t i", i=PAIR),
-                in0=rn_of[r, c][:].rearrange("p t (q i) -> p q t i", i=PAIR),
-                in1=silu_of[r, c][:].rearrange("p t (q i) -> p q t i", i=PAIR),
+                out=gate_of[r][:, c].rearrange("p (q i) t -> p q t i", i=RUN),
+                in0=rn_of[r, c][:].rearrange("p t (q i) -> p q t i", i=RUN),
+                in1=silu_of[r, c][:].rearrange("p t (q i) -> p q t i", i=RUN),
                 op=ALU.mult,
             )
 
@@ -238,6 +249,8 @@ def tile_multiscaleretention_pc_t_kernel(tc, ret, g, gn_weight, gn_bias, w_o, b_
 
             if live(step):
                 transpose_r(step, 1)
+            if live(step + 1):
+                normalise_on_vector(step + 1)
             if live(step - 2):
                 matmuls(step - 2, 0)
                 add_bias(step - 2, 0)
@@ -263,7 +276,7 @@ def tile_multiscaleretention_pc_t_kernel(tc, ret, g, gn_weight, gn_bias, w_o, b_
             if live(step + 1):
                 transpose_g(step + 1, 0)
                 transpose_g(step + 1, 1)
-                normalise(step + 1)
+                normalise_on_scalar(step + 1)
             if live(step):
                 leave_psum(step, 0)
             if live(step + 1):

from contextlib import ExitStack

import concourse.mybir as mybir
from concourse.masks import make_identity

F32 = mybir.dt.float32
BF16 = mybir.dt.bfloat16
U32 = mybir.dt.uint32
U8 = mybir.dt.uint8
FP8X4 = mybir.dt.float8_e4m3fn_x4
ALU = mybir.AluOpType
ACT = mybir.ActivationFunctionType

P = 128
PACK = 4
K_PASS = P * PACK
TOKENS = 4 * 1024
E = 1024
HEADS = 4
HEAD = E // HEADS
EPS = 1e-5
PASSES = E // K_PASS
K_BLOCKS = E // P
TILES = 2
TOK = TILES * P
ROUNDS = TOKENS // TOK
GROUPS = TILES * HEADS
N_BANK = 512
N_HALVES = E // N_BANK
RUN = 4
SCALAR_HEADS = 3
AHEAD = 3

FLOPS = 2 * TOKENS * E * E


def tile_multiscaleretention_pc_t_kernel(tc, ret, g, gn_weight, gn_bias, w_o, b_o, out):
    nc = tc.nc
    ret_rounds = ret.flatten_outer_dims().rearrange("(r p j) c -> r p j c", p=P, j=TILES)
    g_rounds = g.flatten_outer_dims().rearrange("(r p j) c -> r p j c", p=P, j=TILES)
    out_rounds = out.flatten_outer_dims().rearrange("(r p j) c -> r p j c", p=P, j=TILES)
    w_passes = w_o.rearrange("(c t p) n -> c p t n", t=PACK, p=P)

    with ExitStack() as ctx:
        const = ctx.enter_context(tc.tile_pool(name="const", bufs=1))
        w_stage = ctx.enter_context(tc.tile_pool(name="w_stage", bufs=2))
        x_pool = ctx.enter_context(tc.tile_pool(name="x", bufs=AHEAD + 3))
        g_pool = ctx.enter_context(tc.tile_pool(name="g", bufs=4))
        small = ctx.enter_context(tc.tile_pool(name="small", bufs=AHEAD + 2))
        r_pool = ctx.enter_context(tc.tile_pool(name="r", bufs=3))
        t_pool = ctx.enter_context(tc.tile_pool(name="transposed", bufs=4))
        q_pool = ctx.enter_context(tc.tile_pool(name="quantised", bufs=3))
        o_pool = ctx.enter_context(tc.tile_pool(name="o", bufs=3))
        psum_r = ctx.enter_context(tc.psum_pool(name="psum_r", bufs=4))
        psum_g = ctx.enter_context(tc.psum_pool(name="psum_g", bufs=2))
        psum_o = ctx.enter_context(tc.psum_pool(name="psum_o", bufs=2))
        ctx.enter_context(tc.manual_schedule())

        x_of, g_of, stats_of, rstd_of, shift_of, r_of, gate_of, codes_of, scales_of, out_of = (
            {}, {}, {}, {}, {}, {}, {}, {}, {}, {},
        )
        g_bank_of, r_banks_of, silu_of, rn_of, acc_of = {}, {}, {}, {}, {}
        w_raw_of, w_grouped_of = {}, {}

        def load_ret(r):
            x_of[r] = x_pool.tile([P, TILES, E], BF16, name="x_sb")
            nc.sync.dma_start(out=x_of[r][:], in_=ret_rounds[r])

        def load_g(r):
            g_of[r] = g_pool.tile([P, TILES, E], BF16, name="g_sb")
            nc.sync.dma_start(out=g_of[r][:], in_=g_rounds[r])

        def statistics(r):
            stats = small.tile([P, GROUPS, 3], F32, name="stats")
            for j in range(TILES):
                for pair in range(HEADS // 2):
                    i = j * HEADS + 2 * pair
                    nc.vector.bn_stats(
                        out=stats[:, i : i + 2, :].rearrange("p a s -> p (a s)"),
                        in_=x_of[r][:, j, 2 * pair * HEAD : 2 * (pair + 1) * HEAD].rearrange("p (a d) -> p d a", a=2),
                    )
            stats_of[r] = stats

        def scale_and_shift(r):
            mean, count_var = stats_of[r][:, :, 1], stats_of[r][:, :, 2]
            var_eps = small.tile([P, GROUPS], F32, name="var_eps")
            nc.gpsimd.tensor_scalar(
                out=var_eps[:], in0=count_var, scalar1=1.0 / HEAD, scalar2=EPS, op0=ALU.mult, op1=ALU.add
            )
            minus_mean = small.tile([P, GROUPS], F32, name="minus_mean")
            nc.gpsimd.tensor_scalar(out=minus_mean[:], in0=mean, scalar1=-1.0, scalar2=0.0, op0=ALU.mult, op1=ALU.add)
            rstd_of[r] = small.tile([P, GROUPS], F32, name="rstd")
            nc.gpsimd.tensor_tensor(out=rstd_of[r][:], in0=var_eps[:], in1=minus_half[:], op=ALU.pow)
            shift_of[r] = small.tile([P, GROUPS], F32, name="shift")
            nc.gpsimd.tensor_tensor(out=shift_of[r][:], in0=minus_mean[:], in1=rstd_of[r][:], op=ALU.mult)

        def normalise_on_vector(r):
            r_of[r] = r_pool.tile([P, TILES, E], F32, name="r_sb")
            for j in range(TILES):
                for h in range(SCALAR_HEADS, HEADS):
                    i = j * HEADS + h
                    cols = slice(h * HEAD, (h + 1) * HEAD)
                    nc.vector.tensor_scalar(
                        out=r_of[r][:, j, cols], in0=x_of[r][:, j, cols],
                        scalar1=stats_of[r][:, i, 1:2], scalar2=rstd_of[r][:, i : i + 1],
                        op0=ALU.subtract, op1=ALU.mult,
                    )

        def normalise_on_scalar(r):
            for j in range(TILES):
                for h in range(SCALAR_HEADS):
                    i = j * HEADS + h
                    cols = slice(h * HEAD, (h + 1) * HEAD)
                    nc.scalar.activation(
                        out=r_of[r][:, j, cols], in_=x_of[r][:, j, cols], func=ACT.Identity,
                        scale=rstd_of[r][:, i : i + 1], bias=shift_of[r][:, i : i + 1],
                    )

        def transpose_g(r, c):
            g_bank = psum_g.tile([P, PACK, TOK], BF16, name="g_bank")
            for t in range(PACK):
                m = c * PACK + t
                for j in range(TILES):
                    nc.tensor.transpose(
                        g_bank[:, t, j * P : (j + 1) * P], g_of[r][:, j, m * P : (m + 1) * P], ident_bf16[:]
                    )
            g_bank_of[r, c] = g_bank

        def transpose_r(r, c):
            r_banks_of[r, c] = []
            for half in range(PACK // 2):
                r_bank = psum_r.tile([P, 2, TOK], F32, name="r_bank")
                for i in range(2):
                    m = c * PACK + 2 * half + i
                    for j in range(TILES):
                        nc.tensor.transpose(
                            r_bank[:, i, j * P : (j + 1) * P], r_of[r][:, j, m * P : (m + 1) * P], ident_f32[:]
                        )
                r_banks_of[r, c].append(r_bank)

        def leave_psum(r, c):
            silu_of[r, c] = t_pool.tile([P, PACK, TOK], F32, name="silu_t")
            nc.scalar.activation(out=silu_of[r, c][:], in_=g_bank_of[r, c][:], func=ACT.Silu)
            rn_of[r, c] = t_pool.tile([P, PACK, TOK], F32, name="rn_t")
            for t in range(PACK):
                m = c * PACK + t
                nc.scalar.activation(
                    out=rn_of[r, c][:, t, :], in_=r_banks_of[r, c][t // 2][:, t % 2, :], func=ACT.Identity,
                    scale=weight_col[:, m : m + 1], bias=bias_col[:, m : m + 1],
                )

        def product(r, c):
            if c == 0:
                gate_of[r] = q_pool.tile([P, PASSES, TOK, PACK], BF16, name="gate", align_bytes=64)
            nc.vector.tensor_tensor(
                out=gate_of[r][:, c].rearrange("p (q i) t -> p q t i", i=RUN),
                in0=rn_of[r, c][:].rearrange("p t (q i) -> p q t i", i=RUN),
                in1=silu_of[r, c][:].rearrange("p t (q i) -> p q t i", i=RUN),
                op=ALU.mult,
            )

        def quantise(r):
            codes_of[r] = q_pool.tile([P, PASSES, TOK], U32, name="codes", align_bytes=64)
            scales_of[r] = q_pool.tile([P, PASSES, TOK], U8, name="scales", align_bytes=64)
            nc.vector.quantize_mx(
                out=codes_of[r][:].rearrange("p c k -> p (c k)").bitcast(FP8X4),
                scales=scales_of[r][:].rearrange("p c k -> p (c k)"),
                in_=gate_of[r][:].rearrange("p c k t -> p (c k t)"),
            )

        def matmuls(r, j):
            tokens = slice(j * P, (j + 1) * P)
            for n in range(N_HALVES):
                n_cols = slice(n * N_BANK, (n + 1) * N_BANK)
                acc_of[r, j, n] = psum_o.tile([P, N_BANK], F32, name="acc")
                for c in range(PASSES):
                    nc.tensor.matmul_mx(
                        out=acc_of[r, j, n][:],
                        lhsT=codes_of[r][:, c, tokens].bitcast(FP8X4),
                        lhsT_scale=scales_of[r][:, c, tokens],
                        rhs=w_codes[:, c, n_cols].bitcast(FP8X4),
                        rhs_scale=w_scales[:, c, n_cols],
                        start=(c == 0),
                        stop=(c == PASSES - 1),
                    )

        def add_bias(r, j):
            if j == 0:
                out_of[r] = o_pool.tile([P, TILES, E], F32, name="out_sb")
            for n in range(N_HALVES):
                n_cols = slice(n * N_BANK, (n + 1) * N_BANK)
                nc.vector.tensor_tensor(
                    out=out_of[r][:, j, n_cols], in0=acc_of[r, j, n][:], in1=b_all[:, n_cols], op=ALU.add
                )

        def store(r):
            nc.sync.dma_start(out=out_rounds[r], in_=out_of[r][:])

        def load_w(c):
            w_raw_of[c] = w_stage.tile([P, PACK, E], BF16, name="w_raw")
            nc.sync.dma_start(out=w_raw_of[c][:], in_=w_passes[c])

        def regroup_w(c):
            w_grouped_of[c] = w_stage.tile([P, E, PACK], BF16, name="w_grouped", align_bytes=64)
            nc.vector.tensor_copy(
                out=w_grouped_of[c][:].rearrange("p (q i) t -> p q t i", i=RUN),
                in_=w_raw_of[c][:].rearrange("p t (q i) -> p q t i", i=RUN),
            )

        def quantise_w(c):
            nc.vector.quantize_mx(
                out=w_codes[:, c, :].bitcast(FP8X4),
                scales=w_scales[:, c, :],
                in_=w_grouped_of[c][:].rearrange("p n t -> p (n t)"),
            )

        ident_f32 = const.tile([P, P], F32, name="ident_f32")
        make_identity(nc, ident_f32[:])
        ident_bf16 = const.tile([P, P], BF16, name="ident_bf16")
        make_identity(nc, ident_bf16[:])
        minus_half = const.tile([P, GROUPS], F32, name="minus_half")
        nc.gpsimd.memset(minus_half[:], -0.5)
        w_codes = const.tile([P, PASSES, E], U32, name="w_codes", align_bytes=64)
        w_scales = const.tile([P, PASSES, E], U8, name="w_scales", align_bytes=64)

        rows = const.tile([P, P], BF16, name="rows")
        nc.vector.memset(rows[:], 0.0)
        nc.scalar.dma_start(out=rows[0:K_BLOCKS, :], in_=gn_weight.rearrange("(m p) -> m p", p=P))
        nc.scalar.dma_start(out=rows[K_BLOCKS : 2 * K_BLOCKS, :], in_=gn_bias.rearrange("(m p) -> m p", p=P))
        cols_bank = psum_g.tile([P, PACK, TOK], BF16, name="g_bank")
        nc.tensor.transpose(cols_bank[:, 0, 0:P], rows[:], ident_bf16[:])
        weight_col = const.tile([P, K_BLOCKS], F32, name="weight_col")
        bias_col = const.tile([P, K_BLOCKS], F32, name="bias_col")

        b_all = const.tile([P, E], BF16, name="b_all")
        nc.scalar.dma_start(out=b_all[:], in_=b_o.partition_broadcast(P))

        def live(r):
            return 0 <= r < ROUNDS

        first_step = -(AHEAD + 2)
        for step in range(first_step, ROUNDS + 2):
            if live(step + AHEAD + 2):
                load_ret(step + AHEAD + 2)
            if live(step + 2):
                load_g(step + 2)
            if 0 <= step - first_step - 2 < PASSES:
                load_w(step - first_step - 2)

            if live(step):
                transpose_r(step, 1)
            if live(step + 1):
                normalise_on_vector(step + 1)
            if live(step - 2):
                matmuls(step - 2, 0)
                add_bias(step - 2, 0)
                matmuls(step - 2, 1)
            if live(step - 1):
                product(step - 1, 1)
            if live(step - 2):
                add_bias(step - 2, 1)
                store(step - 2)
            if live(step - 1):
                quantise(step - 1)
            if live(step + AHEAD):
                statistics(step + AHEAD)
                scale_and_shift(step + AHEAD)
            if step == -AHEAD:
                nc.vector.tensor_copy(out=weight_col[:], in_=cols_bank[:, 0, 0:K_BLOCKS])
                nc.vector.tensor_copy(out=bias_col[:], in_=cols_bank[:, 0, K_BLOCKS : 2 * K_BLOCKS])
            if 0 <= step + 1 < PASSES:
                quantise_w(step + 1)
            if 0 <= step + 2 < PASSES:
                regroup_w(step + 2)

            if live(step + 1):
                transpose_g(step + 1, 0)
                transpose_g(step + 1, 1)
                normalise_on_scalar(step + 1)
            if live(step):
                leave_psum(step, 0)
            if live(step + 1):
                transpose_r(step + 1, 0)
            if live(step):
                product(step, 0)
                leave_psum(step, 1)
